import numpy as np
import ml_dtypes


def mxq(x, axis, fmt="e4m3"):
    dtype, down = {"e4m3": (ml_dtypes.float8_e4m3fn, 7), "e5m2": (ml_dtypes.float8_e5m2, 14)}[fmt]
    v = np.moveaxis(np.asarray(x, np.float32).astype(ml_dtypes.bfloat16).astype(np.float64), axis, -1)
    blocks = v.reshape(v.shape[:-1] + (-1, 32))
    amax = np.abs(blocks).max(-1, keepdims=True)
    byte = np.maximum(np.where(amax > 0, np.frexp(amax)[1] - 1 + 127, 0) - down, 1)
    scale = np.exp2(byte - 127.0)
    codes = (blocks / scale).astype(np.float32).astype(dtype).astype(np.float64)
    return np.moveaxis((codes * scale).reshape(v.shape), -1, axis)


WIDE = False


def mx_kscale(k):
    if not WIDE:
        return np.ones(k)
    levels = np.array([10, -10, 5, -5, 0])
    a = np.random.permutation(np.resize(levels, k // 512 * 4)).reshape(k // 512, 4)
    idx = np.arange(k)
    return np.exp2(a[idx // 512, idx % 128 // 32])


BF16 = ml_dtypes.bfloat16


def bf(x):
    return np.asarray(x, np.float32).astype(BF16)


def f64(x):
    return np.asarray(x).astype(np.float64)


E2M1 = np.array([0.0, 0.5, 1.0, 1.5, 2.0, 3.0, 4.0, 6.0, -0.0, -0.5, -1.0, -1.5, -2.0, -3.0, -4.0, -6.0])


def pack_weight(w, fmt):
    k, n = w.shape
    w = f64(bf(w)).reshape(k // 32, 32, n)
    amax = np.abs(w).max(1)
    if fmt == "e4m3":
        byte = np.frexp(amax)[1] - 1 + 127 - 7
    else:
        mant, ex = np.frexp(amax / 6.0)
        byte = np.where(mant > 0.5, ex, ex - 1) + 127
    byte = np.clip(np.where(amax > 0, byte, 1), 1, 254)
    scaled = (w * np.exp2(127.0 - byte)[:, None, :]).reshape(k, n).astype(np.float32)
    by_word = np.ascontiguousarray(scaled.reshape(k // 512, 128, 4, n).transpose(0, 1, 3, 2))
    if fmt == "e4m3":
        words = by_word.astype(ml_dtypes.float8_e4m3fn).view(np.uint8)
    else:
        c = by_word.astype(ml_dtypes.float4_e2m1fn).view(np.uint8) & 0xF
        words = c[..., 0::2] | (c[..., 1::2] << 4)
    return np.ascontiguousarray(words), np.ascontiguousarray(byte.astype(np.uint8).reshape(k // 512, 16, n))


def unpack_weight(words, scales, fmt):
    g, p, n, _ = words.shape
    if fmt == "e4m3":
        vals = np.ascontiguousarray(words).view(ml_dtypes.float8_e4m3fn).astype(np.float64)
    else:
        nib = np.empty((g, p, n, 4), np.uint8)
        nib[..., 0::2] = words & 0xF
        nib[..., 1::2] = words >> 4
        vals = E2M1[nib]
    vals = vals * np.repeat(np.exp2(scales.astype(np.float64) - 127.0), 8, axis=1)[..., None]
    return vals.transpose(0, 1, 3, 2).reshape(g * 512, n)


B, C, NP, P, HID = 2, 6, 8, 32, 3072
IN_D = C * P * P
SEQ = NP * NP + 1
IMG = NP * P
FMT = "e4m3"


def positional_embedding(seq_len, dim):
    i = np.arange(seq_len)[:, None].astype(np.float64)
    j = np.arange(dim)[None, :].astype(np.float64)
    ang = i / np.power(100000.0, j / dim)
    return np.where(j % 2 == 0, np.sin(ang), np.cos(ang))


def setup_inputs():
    s = mx_kscale(IN_D)
    X = np.random.standard_normal((B, C, NP, P, NP, P)) * s.reshape(1, C, 1, P, 1, P)
    bound = 2.0 / np.sqrt(IN_D)
    w = np.random.uniform(-bound, bound, (HID, IN_D)) / s[None, :]
    words, scales = pack_weight(np.ascontiguousarray(w.T), FMT)
    return {"X": bf(X.reshape(B, C, IMG, IMG)),
            "W_words": words,
            "W_scales": scales,
            "b": bf(np.random.standard_normal(HID) * 0.3),
            "class_token": bf(np.random.uniform(0.0, 1.0, (1, HID))),
            "pos_embed": bf(positional_embedding(SEQ, HID))}


def reference(X, W_words, W_scales, b, class_token, pos_embed):
    nb = X.shape[0]
    patches = f64(X).reshape(nb, C, NP, P, NP, P)
    patches = patches.transpose(0, 2, 4, 1, 3, 5).reshape(nb, NP * NP, IN_D)
    tokens = (mxq(patches, 2, "e4m3") @ unpack_weight(W_words, W_scales, FMT)) + f64(b)
    cls = np.broadcast_to(f64(class_token)[None, :, :], (nb, 1, HID))
    tokens = np.concatenate([cls, tokens], axis=1)
    return tokens * f64(pos_embed)[None, :, :]

@@ -1,0 +1,178 @@
+from contextlib import ExitStack
+
+import concourse.mybir as mybir
+from concourse.masks import make_identity
+
+F32 = mybir.dt.float32
+BF16 = mybir.dt.bfloat16
+I32 = mybir.dt.int32
+U32 = mybir.dt.uint32
+U8 = mybir.dt.uint8
+FP8X4 = mybir.dt.float8_e4m3fn_x4
+ADD = mybir.AluOpType.add
+MULT = mybir.AluOpType.mult
+
+P = 128
+HID = 3072
+GROUPS = 12
+NCH = 512
+CHUNKS = HID // NCH
+MAIN = 10
+
+FLOPS = 2 * 128 * 6144 * 3072
+
+
+def tile_myvit_w_kernel(tc, X, W_words, W_scales, b, class_token, pos_embed, out):
+    nc = tc.nc
+    with ExitStack() as ctx:
+        const = ctx.enter_context(tc.tile_pool(name="const", bufs=1))
+        xpool = ctx.enter_context(tc.tile_pool(name="xpool", bufs=1))
+        wpool = ctx.enter_context(tc.tile_pool(name="wpool", bufs=1))
+        rpool = ctx.enter_context(tc.tile_pool(name="rpool", bufs=4))
+        accp = ctx.enter_context(tc.psum_pool(name="accp", bufs=1))
+        trp = ctx.enter_context(tc.psum_pool(name="trp", bufs=2))
+        ctx.enter_context(tc.manual_schedule())
+
+        raw0 = xpool.tile([P, 4096], BF16, name="raw0")
+        raw1 = xpool.tile([P, 4096], BF16, name="raw1")
+        srt0 = xpool.tile([P, 4096], BF16, name="srt0")
+        srt1 = xpool.tile([P, 4096], BF16, name="srt1")
+        brow = xpool.tile([P, HID], BF16, name="brow", tag="grp", align_bytes=64)
+        planes = const.tile([P, 3, HID], U8, name="planes", align_bytes=64)
+        xcodes = const.tile([P, GROUPS * P], U32, name="xcodes", align_bytes=64)
+        xsc = const.tile([P, GROUPS * P], U8, name="xsc", align_bytes=64)
+        pos_sb = const.tile([P, HID], BF16, name="pos_sb")
+        bb = const.tile([P, HID], BF16, name="bb")
+        ident = const.tile([P, P], F32, name="ident")
+        perm0 = const.tile([P, P], F32, name="perm0")
+        perm1 = const.tile([P, P], F32, name="perm1")
+        ones = const.tile([P, P], BF16, name="ones")
+        ct = const.tile([32, 96], BF16, name="ct")
+        p0 = const.tile([32, 96], BF16, name="p0")
+        cr = const.tile([32, 96], F32, name="cr")
+
+        nc.vector.memset(raw1[:].bitcast(I32), 0)
+        nc.vector.memset(planes[:].rearrange("p a n -> p (a n)").bitcast(I32), 0)
+        nc.vector.memset(brow[:].bitcast(I32), 0)
+        nc.vector.memset(ones[:], 1.0)
+        make_identity(nc, ident[:])
+
+        xr = X.rearrange("b c (r y) x -> (b c r) (y x)", y=16)
+        nc.sync.dma_start(out=raw0[:], in_=xr[0:128, :])
+        nc.sync.dma_start(out=raw1[32:96, :], in_=xr[128:192, :])
+
+        nc.scalar.dma_start(out=ct[:], in_=class_token.rearrange("o (p f) -> (o p) f", p=32))
+        nc.scalar.dma_start(out=p0[:], in_=pos_embed[0:1, :].rearrange("o (p f) -> (o p) f", p=32))
+        nc.scalar.dma_start(out=brow[0:1, :], in_=b.rearrange("(o n) -> o n", o=1))
+
+        for a in range(3):
+            for q in range(4):
+                nc.sync.dma_start(
+                    out=planes[32 * q : 32 * q + 16, a, :].bitcast(I32),
+                    in_=W_scales[4 * a : 4 * a + 4, 4 * q : 4 * q + 4, :].bitcast(I32),
+                )
+        nc.sync.dma_start(out=pos_sb[0:128:2, :], in_=pos_embed[1:65, :])
+        nc.sync.dma_start(out=pos_sb[1:128:2, :], in_=pos_embed[1:65, :])
+
+        wmain = []
+        for g in range(MAIN):
+            w = wpool.tile([P, HID], U32, name="w%d" % g, align_bytes=64)
+            nc.sync.dma_start(
+                out=w[:].bitcast(I32),
+                in_=W_words[g].rearrange("p n t -> p (n t)").bitcast(I32),
+            )
+            wmain.append(w)
+        wtail = []
+        for j in range(CHUNKS):
+            w = wpool.tile([P, GROUPS - MAIN, NCH], U32, name="wt%d" % j, align_bytes=64)
+            nc.sync.dma_start(
+                out=w[:].bitcast(I32),
+                in_=W_words[MAIN:GROUPS, :, NCH * j : NCH * (j + 1), :]
+                .rearrange("g p n t -> p g (n t)")
+                .bitcast(I32),
+            )
+            wtail.append(w)
+
+        nc.vector.tensor_copy(
+            out=perm0[:].rearrange("p (c h y) -> p c h y", c=8, h=2, y=8),
+            in_=ident[:].rearrange("p (c y h) -> p c h y", c=8, y=8, h=2),
+        )
+        nc.vector.tensor_copy(
+            out=perm1[:, 0:64].rearrange("p (c h y) -> p c h y", c=4, h=2, y=8),
+            in_=ident[:, 32:96].rearrange("p (c y h) -> p c h y", c=4, y=8, h=2),
+        )
+        nc.vector.tensor_copy(out=perm1[:, 64:96], in_=ident[:, 0:32])
+        nc.vector.tensor_copy(out=perm1[:, 96:128], in_=ident[:, 96:128])
+
+        nc.gpsimd.tensor_tensor(out=cr[:], in0=ct[:], in1=p0[:], op=MULT)
+        for bi in range(2):
+            nc.scalar.dma_start(
+                out=out[bi, 0:1, :].rearrange("o (p f) -> (o p) f", p=32), in_=cr[:]
+            )
+
+        for j in range(CHUNKS):
+            cols = slice(NCH * j, NCH * (j + 1))
+            ps = trp.tile([P, NCH], F32, name="ps", tag="tr")
+            nc.tensor.matmul(out=ps[:], lhsT=ones[:], rhs=brow[:, cols], start=True, stop=True)
+            nc.scalar.copy(out=bb[:, cols], in_=ps[:])
+
+        for raw, srt in ((raw0, srt0), (raw1, srt1)):
+            nc.vector.tensor_copy(
+                out=srt[:].rearrange("q (g y x) -> q g y x", g=8, y=16, x=32),
+                in_=raw[:].rearrange("q (y g x) -> q g y x", y=16, g=8, x=32),
+            )
+        grouped = xpool.tile([P, GROUPS * P * 4], BF16, name="grouped", tag="grp", align_bytes=64)
+        gw = grouped[:].bitcast(F32).rearrange("p (k x s) -> p k x s", k=96, x=8, s=4)
+        for gx in range(8):
+            ps = trp.tile([P, NCH], F32, name="ps", tag="tr")
+            for u in range(2):
+                for t, (srt, perm) in enumerate(((srt0, perm0), (srt1, perm1))):
+                    slot = 2 * u + t
+                    nc.tensor.transpose(
+                        ps[:, P * slot : P * (slot + 1)],
+                        srt[:].bitcast(F32)[:, 256 * gx + u : 256 * (gx + 1) : 2],
+                        perm[:],
+                    )
+            src = (
+                ps[:]
+                .rearrange("p (u r) -> p u r", u=2)[:, :, 0:192]
+                .rearrange("p u (b k) -> p k b u", b=2)
+            )
+            dst = gw[:, :, gx, :].rearrange("p k (b u) -> p k b u", b=2)
+            if (gx // 2) % 2 == 0:
+                nc.vector.tensor_copy(out=dst, in_=src)
+            else:
+                nc.scalar.copy(out=dst, in_=src)
+        for i in range(3):
+            nc.vector.quantize_mx(
+                out=xcodes[:, 512 * i : 512 * (i + 1)].bitcast(FP8X4),
+                scales=xsc[:, 512 * i : 512 * (i + 1)],
+                in_=grouped[:, 2048 * i : 2048 * (i + 1)],
+            )
+
+        acc = [accp.tile([P, NCH], F32, name="acc%d" % j) for j in range(CHUNKS)]
+
+        def mx_pass(g, j, rhs):
+            nc.tensor.matmul_mx(
+                out=acc[j][:],
+                lhsT=xcodes[:, P * g : P * (g + 1)].bitcast(FP8X4),
+                lhsT_scale=xsc[:, P * g : P * (g + 1)],
+                rhs=rhs.bitcast(FP8X4),
+                rhs_scale=planes[4 * (g % 4) : P, g // 4, NCH * j : NCH * (j + 1)],
+                start=(g == 0),
+                stop=(g == GROUPS - 1),
+            )
+
+        for g in range(MAIN):
+            for j in range(CHUNKS):
+                mx_pass(g, j, wmain[g][:, NCH * j : NCH * (j + 1)])
+
+        out_tok = out[:, 1:65, :].rearrange("b t n -> t b n")
+        for j in range(CHUNKS):
+            cols = slice(NCH * j, NCH * (j + 1))
+            for g in range(MAIN, GROUPS):
+                mx_pass(g, j, wtail[j][:, g - MAIN, :])
+            res = rpool.tile([P, NCH], F32, name="res")
+            nc.vector.tensor_tensor(out=res[:], in0=acc[j][:], in1=bb[:, cols], op=ADD)
+            nc.vector.tensor_tensor(out=res[:], in0=res[:], in1=pos_sb[:, cols], op=MULT)
+            nc.sync.dma_start(out=out_tok[:, :, cols], in_=res[:])

@@ -51,8 +51,8 @@ def tile_myvit_w_kernel(tc, X, W_words, W_scales, b, class_token, pos_embed, out
         p0 = const.tile([32, 96], BF16, name="p0")
         cr = const.tile([32, 96], F32, name="cr")
 
-        nc.vector.memset(raw1[:].bitcast(I32), 0)
         nc.vector.memset(planes[:].rearrange("p a n -> p (a n)").bitcast(I32), 0)
+        nc.vector.memset(raw1[:].bitcast(I32), 0)
         nc.vector.memset(brow[:].bitcast(I32), 0)
         nc.vector.memset(ones[:], 1.0)
         make_identity(nc, ident[:])
@@ -67,9 +67,9 @@ def tile_myvit_w_kernel(tc, X, W_words, W_scales, b, class_token, pos_embed, out
 
         for a in range(3):
             for q in range(4):
-                nc.sync.dma_start(
-                    out=planes[32 * q : 32 * q + 16, a, :].bitcast(I32),
-                    in_=W_scales[4 * a : 4 * a + 4, 4 * q : 4 * q + 4, :].bitcast(I32),
+                nc.gpsimd.dma_start(
+                    out=planes[32 * q : 32 * q + 16, a, :].bitcast(F32),
+                    in_=W_scales[4 * a : 4 * a + 4, 4 * q : 4 * q + 4, :].bitcast(F32),
                 )
         nc.sync.dma_start(out=pos_sb[0:128:2, :], in_=pos_embed[1:65, :])
         nc.sync.dma_start(out=pos_sb[1:128:2, :], in_=pos_embed[1:65, :])
@@ -104,7 +104,7 @@ def tile_myvit_w_kernel(tc, X, W_words, W_scales, b, class_token, pos_embed, out
         nc.vector.tensor_copy(out=perm1[:, 64:96], in_=ident[:, 0:32])
         nc.vector.tensor_copy(out=perm1[:, 96:128], in_=ident[:, 96:128])
 
-        nc.gpsimd.tensor_tensor(out=cr[:], in0=ct[:], in1=p0[:], op=MULT)
+        nc.vector.tensor_tensor(out=cr[:], in0=ct[:], in1=p0[:], op=MULT)
         for bi in range(2):
             nc.scalar.dma_start(
                 out=out[bi, 0:1, :].rearrange("o (p f) -> (o p) f", p=32), in_=cr[:]

@@ -17,7 +17,7 @@ HID = 3072
 GROUPS = 12
 NCH = 512
 CHUNKS = HID // NCH
-MAIN = 10
+MAIN = 9
 
 FLOPS = 2 * 128 * 6144 * 3072
 
@@ -51,8 +51,8 @@ def tile_myvit_w_kernel(tc, X, W_words, W_scales, b, class_token, pos_embed, out
         p0 = const.tile([32, 96], BF16, name="p0")
         cr = const.tile([32, 96], F32, name="cr")
 
-        nc.vector.memset(planes[:].rearrange("p a n -> p (a n)").bitcast(I32), 0)
         nc.vector.memset(raw1[:].bitcast(I32), 0)
+        nc.vector.memset(planes[:].rearrange("p a n -> p (a n)").bitcast(I32), 0)
         nc.vector.memset(brow[:].bitcast(I32), 0)
         nc.vector.memset(ones[:], 1.0)
         make_identity(nc, ident[:])
@@ -67,9 +67,9 @@ def tile_myvit_w_kernel(tc, X, W_words, W_scales, b, class_token, pos_embed, out
 
         for a in range(3):
             for q in range(4):
-                nc.gpsimd.dma_start(
-                    out=planes[32 * q : 32 * q + 16, a, :].bitcast(F32),
-                    in_=W_scales[4 * a : 4 * a + 4, 4 * q : 4 * q + 4, :].bitcast(F32),
+                nc.sync.dma_start(
+                    out=planes[32 * q : 32 * q + 16, a, :].bitcast(I32),
+                    in_=W_scales[4 * a : 4 * a + 4, 4 * q : 4 * q + 4, :].bitcast(I32),
                 )
         nc.sync.dma_start(out=pos_sb[0:128:2, :], in_=pos_embed[1:65, :])
         nc.sync.dma_start(out=pos_sb[1:128:2, :], in_=pos_embed[1:65, :])
@@ -104,7 +104,7 @@ def tile_myvit_w_kernel(tc, X, W_words, W_scales, b, class_token, pos_embed, out
         nc.vector.tensor_copy(out=perm1[:, 64:96], in_=ident[:, 0:32])
         nc.vector.tensor_copy(out=perm1[:, 96:128], in_=ident[:, 96:128])
 
-        nc.vector.tensor_tensor(out=cr[:], in0=ct[:], in1=p0[:], op=MULT)
+        nc.gpsimd.tensor_tensor(out=cr[:], in0=ct[:], in1=p0[:], op=MULT)
         for bi in range(2):
             nc.scalar.dma_start(
                 out=out[bi, 0:1, :].rearrange("o (p f) -> (o p) f", p=32), in_=cr[:]

@@ -16,8 +16,11 @@ P = 128
 HID = 3072
 GROUPS = 12
 NCH = 512
-CHUNKS = HID // NCH
-MAIN = 9
+
+UNITS = ((0, 512), (512, 512), (1024, 512), (1536, 512), (2048, 512), (2560, 256), (2816, 256))
+FIRST = (10, 10, 10, 10, 9, 9, 9)
+FULL = 9
+PART = 2048
 
 FLOPS = 2 * 128 * 6144 * 3072
 
@@ -29,15 +32,15 @@ def tile_myvit_w_kernel(tc, X, W_words, W_scales, b, class_token, pos_embed, out
         xpool = ctx.enter_context(tc.tile_pool(name="xpool", bufs=1))
         wpool = ctx.enter_context(tc.tile_pool(name="wpool", bufs=1))
         rpool = ctx.enter_context(tc.tile_pool(name="rpool", bufs=4))
-        accp = ctx.enter_context(tc.psum_pool(name="accp", bufs=1))
-        trp = ctx.enter_context(tc.psum_pool(name="trp", bufs=2))
+        psum = ctx.enter_context(tc.psum_pool(name="psum", bufs=1))
         ctx.enter_context(tc.manual_schedule())
 
         raw0 = xpool.tile([P, 4096], BF16, name="raw0")
         raw1 = xpool.tile([P, 4096], BF16, name="raw1")
         srt0 = xpool.tile([P, 4096], BF16, name="srt0")
         srt1 = xpool.tile([P, 4096], BF16, name="srt1")
-        brow = xpool.tile([P, HID], BF16, name="brow", tag="grp", align_bytes=64)
+        aux = xpool.tile([P, HID], BF16, name="aux")
+        grouped = xpool.tile([P, GROUPS * P * 4], BF16, name="grouped", align_bytes=64)
         planes = const.tile([P, 3, HID], U8, name="planes", align_bytes=64)
         xcodes = const.tile([P, GROUPS * P], U32, name="xcodes", align_bytes=64)
         xsc = const.tile([P, GROUPS * P], U8, name="xsc", align_bytes=64)
@@ -46,52 +49,53 @@ def tile_myvit_w_kernel(tc, X, W_words, W_scales, b, class_token, pos_embed, out
         ident = const.tile([P, P], F32, name="ident")
         perm0 = const.tile([P, P], F32, name="perm0")
         perm1 = const.tile([P, P], F32, name="perm1")
-        ones = const.tile([P, P], BF16, name="ones")
+        selp = const.tile([P, P], BF16, name="selp")
+        selb = const.tile([P, P], BF16, name="selb")
         ct = const.tile([32, 96], BF16, name="ct")
         p0 = const.tile([32, 96], BF16, name="p0")
         cr = const.tile([32, 96], F32, name="cr")
 
-        nc.vector.memset(raw1[:].bitcast(I32), 0)
         nc.vector.memset(planes[:].rearrange("p a n -> p (a n)").bitcast(I32), 0)
-        nc.vector.memset(brow[:].bitcast(I32), 0)
-        nc.vector.memset(ones[:], 1.0)
+        nc.vector.memset(raw1[:].bitcast(I32), 0)
+        nc.vector.memset(aux[0:32, :].bitcast(I32), 0)
+        nc.vector.memset(aux[96:128, :].bitcast(I32), 0)
         make_identity(nc, ident[:])
+
+        def load_scales(a, q):
+            nc.sync.dma_start(
+                out=planes[32 * q : 32 * q + 16, a, :].bitcast(I32),
+                in_=W_scales[4 * a : 4 * a + 4, 4 * q : 4 * q + 4, :].bitcast(I32),
+            )
+
+        def load_words(name, g0, g1, c0, c1):
+            w = wpool.tile([P, g1 - g0, c1 - c0], U32, name=name, align_bytes=64)
+            nc.sync.dma_start(
+                out=w[:].bitcast(I32),
+                in_=W_words[g0:g1, :, c0:c1, :].rearrange("g p n t -> p g (n t)").bitcast(I32),
+            )
+            return w
 
         xr = X.rearrange("b c (r y) x -> (b c r) (y x)", y=16)
         nc.sync.dma_start(out=raw0[:], in_=xr[0:128, :])
-        nc.sync.dma_start(out=raw1[32:96, :], in_=xr[128:192, :])
-
-        nc.scalar.dma_start(out=ct[:], in_=class_token.rearrange("o (p f) -> (o p) f", p=32))
-        nc.scalar.dma_start(out=p0[:], in_=pos_embed[0:1, :].rearrange("o (p f) -> (o p) f", p=32))
-        nc.scalar.dma_start(out=brow[0:1, :], in_=b.rearrange("(o n) -> o n", o=1))
-
         for a in range(3):
-            for q in range(4):
-                nc.sync.dma_start(
-                    out=planes[32 * q : 32 * q + 16, a, :].bitcast(I32),
-                    in_=W_scales[4 * a : 4 * a + 4, 4 * q : 4 * q + 4, :].bitcast(I32),
-                )
-        nc.sync.dma_start(out=pos_sb[0:128:2, :], in_=pos_embed[1:65, :])
-        nc.sync.dma_start(out=pos_sb[1:128:2, :], in_=pos_embed[1:65, :])
-
-        wmain = []
-        for g in range(MAIN):
-            w = wpool.tile([P, HID], U32, name="w%d" % g, align_bytes=64)
-            nc.sync.dma_start(
-                out=w[:].bitcast(I32),
-                in_=W_words[g].rearrange("p n t -> p (n t)").bitcast(I32),
-            )
-            wmain.append(w)
-        wtail = []
-        for j in range(CHUNKS):
-            w = wpool.tile([P, GROUPS - MAIN, NCH], U32, name="wt%d" % j, align_bytes=64)
-            nc.sync.dma_start(
-                out=w[:].bitcast(I32),
-                in_=W_words[MAIN:GROUPS, :, NCH * j : NCH * (j + 1), :]
-                .rearrange("g p n t -> p g (n t)")
-                .bitcast(I32),
-            )
-            wtail.append(w)
+            for q in (0, 1):
+                load_scales(a, q)
+        nc.sync.dma_start(out=raw1[32:96, :], in_=xr[128:192, :])
+        for a in range(3):
+            for q in (2, 3):
+                load_scales(a, q)
+        nc.sync.dma_start(out=aux[32:96, :], in_=pos_embed[1:65, :])
+        nc.sync.dma_start(out=aux[0:1, :], in_=b.rearrange("(o n) -> o n", o=1))
+        wfull = [load_words("w0", 0, 1, 0, HID)]
+        nc.sync.dma_start(out=ct[:], in_=class_token.rearrange("o (p f) -> (o p) f", p=32))
+        nc.sync.dma_start(out=p0[:], in_=pos_embed[0:1, :].rearrange("o (p f) -> (o p) f", p=32))
+        for g in range(1, FULL):
+            wfull.append(load_words("w%d" % g, g, g + 1, 0, HID))
+        wpart = load_words("wpart", FULL, FULL + 1, 0, PART)
+        wunit = [
+            load_words("wu%d" % u, FIRST[u], GROUPS, c0, c0 + width)
+            for u, (c0, width) in enumerate(UNITS)
+        ]
 
         nc.vector.tensor_copy(
             out=perm0[:].rearrange("p (c h y) -> p c h y", c=8, h=2, y=8),
@@ -103,28 +107,20 @@ def tile_myvit_w_kernel(tc, X, W_words, W_scales, b, class_token, pos_embed, out
         )
         nc.vector.tensor_copy(out=perm1[:, 64:96], in_=ident[:, 0:32])
         nc.vector.tensor_copy(out=perm1[:, 96:128], in_=ident[:, 96:128])
-
-        nc.gpsimd.tensor_tensor(out=cr[:], in0=ct[:], in1=p0[:], op=MULT)
-        for bi in range(2):
-            nc.scalar.dma_start(
-                out=out[bi, 0:1, :].rearrange("o (p f) -> (o p) f", p=32), in_=cr[:]
-            )
-
-        for j in range(CHUNKS):
-            cols = slice(NCH * j, NCH * (j + 1))
-            ps = trp.tile([P, NCH], F32, name="ps", tag="tr")
-            nc.tensor.matmul(out=ps[:], lhsT=ones[:], rhs=brow[:, cols], start=True, stop=True)
-            nc.scalar.copy(out=bb[:, cols], in_=ps[:])
+        nc.vector.tensor_copy(
+            out=selp[:].rearrange("p (t b) -> p t b", b=2),
+            in_=ident[:, 32:96].unsqueeze(2).to_broadcast([P, 64, 2]),
+        )
+        nc.vector.tensor_copy(out=selb[:], in_=ident[:, 0:1].to_broadcast([P, P]))
 
         for raw, srt in ((raw0, srt0), (raw1, srt1)):
             nc.vector.tensor_copy(
                 out=srt[:].rearrange("q (g y x) -> q g y x", g=8, y=16, x=32),
                 in_=raw[:].rearrange("q (y g x) -> q g y x", y=16, g=8, x=32),
             )
-        grouped = xpool.tile([P, GROUPS * P * 4], BF16, name="grouped", tag="grp", align_bytes=64)
         gw = grouped[:].bitcast(F32).rearrange("p (k x s) -> p k x s", k=96, x=8, s=4)
         for gx in range(8):
-            ps = trp.tile([P, NCH], F32, name="ps", tag="tr")
+            ps = psum.tile([P, NCH], F32, name="px%d" % gx, tag="bk%d" % gx)
             for u in range(2):
                 for t, (srt, perm) in enumerate(((srt0, perm0), (srt1, perm1))):
                     slot = 2 * u + t
@@ -150,29 +146,52 @@ def tile_myvit_w_kernel(tc, X, W_words, W_scales, b, class_token, pos_embed, out
                 in_=grouped[:, 2048 * i : 2048 * (i + 1)],
             )
 
-        acc = [accp.tile([P, NCH], F32, name="acc%d" % j) for j in range(CHUNKS)]
+        for i in range(12):
+            cols = slice(NCH * (i // 2), NCH * (i // 2 + 1))
+            ps = psum.tile([P, NCH], F32, name="pa%d" % i, tag="bk%d" % (i % 8))
+            if i % 2 == 0:
+                nc.tensor.matmul(out=ps[:], lhsT=selb[:], rhs=aux[:, cols], start=True, stop=True)
+                nc.scalar.copy(out=bb[:, cols], in_=ps[:])
+            else:
+                nc.tensor.matmul(out=ps[:], lhsT=selp[:], rhs=aux[:, cols], start=True, stop=True)
+                nc.vector.tensor_copy(out=pos_sb[:, cols], in_=ps[:])
 
-        def mx_pass(g, j, rhs):
+        nc.vector.tensor_tensor(out=cr[:], in0=ct[:], in1=p0[:], op=MULT)
+        for bi in range(2):
+            nc.scalar.dma_start(
+                out=out[bi, 0:1, :].rearrange("o (p f) -> (o p) f", p=32), in_=cr[:]
+            )
+
+        acc = [
+            psum.tile([P, width], F32, name="acc%d" % u, tag="bk%d" % u)
+            for u, (c0, width) in enumerate(UNITS)
+        ]
+
+        def mx_pass(g, u, rhs):
+            c0, width = UNITS[u]
             nc.tensor.matmul_mx(
-                out=acc[j][:],
+                out=acc[u][:],
                 lhsT=xcodes[:, P * g : P * (g + 1)].bitcast(FP8X4),
                 lhsT_scale=xsc[:, P * g : P * (g + 1)],
                 rhs=rhs.bitcast(FP8X4),
-                rhs_scale=planes[4 * (g % 4) : P, g // 4, NCH * j : NCH * (j + 1)],
+                rhs_scale=planes[4 * (g % 4) : P, g // 4, c0 : c0 + width],
                 start=(g == 0),
                 stop=(g == GROUPS - 1),
             )
 
-        for g in range(MAIN):
-            for j in range(CHUNKS):
-                mx_pass(g, j, wmain[g][:, NCH * j : NCH * (j + 1)])
+        for g in range(FULL):
+            for u, (c0, width) in enumerate(UNITS):
+                mx_pass(g, u, wfull[g][:, 0, c0 : c0 + width])
+        for u, (c0, width) in enumerate(UNITS):
+            if FIRST[u] > FULL:
+                mx_pass(FULL, u, wpart[:, 0, c0 : c0 + width])
 
         out_tok = out[:, 1:65, :].rearrange("b t n -> t b n")
-        for j in range(CHUNKS):
-            cols = slice(NCH * j, NCH * (j + 1))
-            for g in range(MAIN, GROUPS):
-                mx_pass(g, j, wtail[j][:, g - MAIN, :])
-            res = rpool.tile([P, NCH], F32, name="res")
-            nc.vector.tensor_tensor(out=res[:], in0=acc[j][:], in1=bb[:, cols], op=ADD)
+        for u, (c0, width) in enumerate(UNITS):
+            cols = slice(c0, c0 + width)
+            for g in range(FIRST[u], GROUPS):
+                mx_pass(g, u, wunit[u][:, g - FIRST[u], :])
+            res = rpool.tile([P, width], F32, name="res", tag="res")
+            nc.vector.tensor_tensor(out=res[:], in0=acc[u][:], in1=bb[:, cols], op=ADD)
             nc.vector.tensor_tensor(out=res[:], in0=res[:], in1=pos_sb[:, cols], op=MULT)
             nc.sync.dma_start(out=out_tok[:, :, cols], in_=res[:])

@@ -16,11 +16,8 @@ P = 128
 HID = 3072
 GROUPS = 12
 NCH = 512
-
-UNITS = ((0, 512), (512, 512), (1024, 512), (1536, 512), (2048, 512), (2560, 256), (2816, 256))
-FIRST = (10, 10, 10, 10, 9, 9, 9)
-FULL = 9
-PART = 2048
+CHUNKS = HID // NCH
+MAIN = 10
 
 FLOPS = 2 * 128 * 6144 * 3072
 
@@ -32,15 +29,15 @@ def tile_myvit_w_kernel(tc, X, W_words, W_scales, b, class_token, pos_embed, out
         xpool = ctx.enter_context(tc.tile_pool(name="xpool", bufs=1))
         wpool = ctx.enter_context(tc.tile_pool(name="wpool", bufs=1))
         rpool = ctx.enter_context(tc.tile_pool(name="rpool", bufs=4))
-        psum = ctx.enter_context(tc.psum_pool(name="psum", bufs=1))
+        accp = ctx.enter_context(tc.psum_pool(name="accp", bufs=1))
+        trp = ctx.enter_context(tc.psum_pool(name="trp", bufs=2))
         ctx.enter_context(tc.manual_schedule())
 
         raw0 = xpool.tile([P, 4096], BF16, name="raw0")
         raw1 = xpool.tile([P, 4096], BF16, name="raw1")
         srt0 = xpool.tile([P, 4096], BF16, name="srt0")
         srt1 = xpool.tile([P, 4096], BF16, name="srt1")
-        aux = xpool.tile([P, HID], BF16, name="aux")
-        grouped = xpool.tile([P, GROUPS * P * 4], BF16, name="grouped", align_bytes=64)
+        brow = xpool.tile([P, HID], BF16, name="brow")
         planes = const.tile([P, 3, HID], U8, name="planes", align_bytes=64)
         xcodes = const.tile([P, GROUPS * P], U32, name="xcodes", align_bytes=64)
         xsc = const.tile([P, GROUPS * P], U8, name="xsc", align_bytes=64)
@@ -49,53 +46,52 @@ def tile_myvit_w_kernel(tc, X, W_words, W_scales, b, class_token, pos_embed, out
         ident = const.tile([P, P], F32, name="ident")
         perm0 = const.tile([P, P], F32, name="perm0")
         perm1 = const.tile([P, P], F32, name="perm1")
-        selp = const.tile([P, P], BF16, name="selp")
-        selb = const.tile([P, P], BF16, name="selb")
+        ones = const.tile([P, P], BF16, name="ones")
         ct = const.tile([32, 96], BF16, name="ct")
         p0 = const.tile([32, 96], BF16, name="p0")
         cr = const.tile([32, 96], F32, name="cr")
 
         nc.vector.memset(planes[:].rearrange("p a n -> p (a n)").bitcast(I32), 0)
         nc.vector.memset(raw1[:].bitcast(I32), 0)
-        nc.vector.memset(aux[0:32, :].bitcast(I32), 0)
-        nc.vector.memset(aux[96:128, :].bitcast(I32), 0)
+        nc.vector.memset(brow[:].bitcast(I32), 0)
+        nc.vector.memset(ones[:], 1.0)
         make_identity(nc, ident[:])
-
-        def load_scales(a, q):
-            nc.sync.dma_start(
-                out=planes[32 * q : 32 * q + 16, a, :].bitcast(I32),
-                in_=W_scales[4 * a : 4 * a + 4, 4 * q : 4 * q + 4, :].bitcast(I32),
-            )
-
-        def load_words(name, g0, g1, c0, c1):
-            w = wpool.tile([P, g1 - g0, c1 - c0], U32, name=name, align_bytes=64)
-            nc.sync.dma_start(
-                out=w[:].bitcast(I32),
-                in_=W_words[g0:g1, :, c0:c1, :].rearrange("g p n t -> p g (n t)").bitcast(I32),
-            )
-            return w
 
         xr = X.rearrange("b c (r y) x -> (b c r) (y x)", y=16)
         nc.sync.dma_start(out=raw0[:], in_=xr[0:128, :])
-        for a in range(3):
-            for q in (0, 1):
-                load_scales(a, q)
         nc.sync.dma_start(out=raw1[32:96, :], in_=xr[128:192, :])
+
+        nc.scalar.dma_start(out=ct[:], in_=class_token.rearrange("o (p f) -> (o p) f", p=32))
+        nc.scalar.dma_start(out=p0[:], in_=pos_embed[0:1, :].rearrange("o (p f) -> (o p) f", p=32))
+
         for a in range(3):
-            for q in (2, 3):
-                load_scales(a, q)
-        nc.sync.dma_start(out=aux[32:96, :], in_=pos_embed[1:65, :])
-        nc.sync.dma_start(out=aux[0:1, :], in_=b.rearrange("(o n) -> o n", o=1))
-        wfull = [load_words("w0", 0, 1, 0, HID)]
-        nc.sync.dma_start(out=ct[:], in_=class_token.rearrange("o (p f) -> (o p) f", p=32))
-        nc.sync.dma_start(out=p0[:], in_=pos_embed[0:1, :].rearrange("o (p f) -> (o p) f", p=32))
-        for g in range(1, FULL):
-            wfull.append(load_words("w%d" % g, g, g + 1, 0, HID))
-        wpart = load_words("wpart", FULL, FULL + 1, 0, PART)
-        wunit = [
-            load_words("wu%d" % u, FIRST[u], GROUPS, c0, c0 + width)
-            for u, (c0, width) in enumerate(UNITS)
-        ]
+            for q in range(4):
+                nc.scalar.dma_start(
+                    out=planes[32 * q : 32 * q + 16, a, :].bitcast(F32),
+                    in_=W_scales[4 * a : 4 * a + 4, 4 * q : 4 * q + 4, :].bitcast(F32),
+                )
+        nc.scalar.dma_start(out=brow[0:1, :], in_=b.rearrange("(o n) -> o n", o=1))
+        nc.sync.dma_start(out=pos_sb[0:128:2, :], in_=pos_embed[1:65, :])
+        nc.sync.dma_start(out=pos_sb[1:128:2, :], in_=pos_embed[1:65, :])
+
+        wmain = []
+        for g in range(MAIN):
+            w = wpool.tile([P, HID], U32, name="w%d" % g, align_bytes=64)
+            nc.sync.dma_start(
+                out=w[:].bitcast(I32),
+                in_=W_words[g].rearrange("p n t -> p (n t)").bitcast(I32),
+            )
+            wmain.append(w)
+        wtail = []
+        for j in range(CHUNKS):
+            w = wpool.tile([P, GROUPS - MAIN, NCH], U32, name="wt%d" % j, align_bytes=64)
+            nc.sync.dma_start(
+                out=w[:].bitcast(I32),
+                in_=W_words[MAIN:GROUPS, :, NCH * j : NCH * (j + 1), :]
+                .rearrange("g p n t -> p g (n t)")
+                .bitcast(I32),
+            )
+            wtail.append(w)
 
         nc.vector.tensor_copy(
             out=perm0[:].rearrange("p (c h y) -> p c h y", c=8, h=2, y=8),
@@ -107,20 +103,22 @@ def tile_myvit_w_kernel(tc, X, W_words, W_scales, b, class_token, pos_embed, out
         )
         nc.vector.tensor_copy(out=perm1[:, 64:96], in_=ident[:, 0:32])
         nc.vector.tensor_copy(out=perm1[:, 96:128], in_=ident[:, 96:128])
-        nc.vector.tensor_copy(
-            out=selp[:].rearrange("p (t b) -> p t b", b=2),
-            in_=ident[:, 32:96].unsqueeze(2).to_broadcast([P, 64, 2]),
-        )
-        nc.vector.tensor_copy(out=selb[:], in_=ident[:, 0:1].to_broadcast([P, P]))
+
+        nc.gpsimd.tensor_tensor(out=cr[:], in0=ct[:], in1=p0[:], op=MULT)
+        for bi in range(2):
+            nc.scalar.dma_start(
+                out=out[bi, 0:1, :].rearrange("o (p f) -> (o p) f", p=32), in_=cr[:]
+            )
 
         for raw, srt in ((raw0, srt0), (raw1, srt1)):
             nc.vector.tensor_copy(
                 out=srt[:].rearrange("q (g y x) -> q g y x", g=8, y=16, x=32),
                 in_=raw[:].rearrange("q (y g x) -> q g y x", y=16, g=8, x=32),
             )
+        grouped = xpool.tile([P, GROUPS * P * 4], BF16, name="grouped", align_bytes=64)
         gw = grouped[:].bitcast(F32).rearrange("p (k x s) -> p k x s", k=96, x=8, s=4)
         for gx in range(8):
-            ps = psum.tile([P, NCH], F32, name="px%d" % gx, tag="bk%d" % gx)
+            ps = trp.tile([P, NCH], F32, name="ps", tag="tr")
             for u in range(2):
                 for t, (srt, perm) in enumerate(((srt0, perm0), (srt1, perm1))):
                     slot = 2 * u + t
@@ -135,10 +133,7 @@ def tile_myvit_w_kernel(tc, X, W_words, W_scales, b, class_token, pos_embed, out
                 .rearrange("p u (b k) -> p k b u", b=2)
             )
             dst = gw[:, :, gx, :].rearrange("p k (b u) -> p k b u", b=2)
-            if (gx // 2) % 2 == 0:
-                nc.vector.tensor_copy(out=dst, in_=src)
-            else:
-                nc.scalar.copy(out=dst, in_=src)
+            nc.vector.tensor_copy(out=dst, in_=src)
         for i in range(3):
             nc.vector.quantize_mx(
                 out=xcodes[:, 512 * i : 512 * (i + 1)].bitcast(FP8X4),
@@ -146,52 +141,34 @@ def tile_myvit_w_kernel(tc, X, W_words, W_scales, b, class_token, pos_embed, out
                 in_=grouped[:, 2048 * i : 2048 * (i + 1)],
             )
 
-        for i in range(12):
-            cols = slice(NCH * (i // 2), NCH * (i // 2 + 1))
-            ps = psum.tile([P, NCH], F32, name="pa%d" % i, tag="bk%d" % (i % 8))
-            if i % 2 == 0:
-                nc.tensor.matmul(out=ps[:], lhsT=selb[:], rhs=aux[:, cols], start=True, stop=True)
-                nc.scalar.copy(out=bb[:, cols], in_=ps[:])
-            else:
-                nc.tensor.matmul(out=ps[:], lhsT=selp[:], rhs=aux[:, cols], start=True, stop=True)
-                nc.vector.tensor_copy(out=pos_sb[:, cols], in_=ps[:])
+        acc = [accp.tile([P, NCH], F32, name="acc%d" % j) for j in range(CHUNKS)]
 
-        nc.vector.tensor_tensor(out=cr[:], in0=ct[:], in1=p0[:], op=MULT)
-        for bi in range(2):
-            nc.scalar.dma_start(
-                out=out[bi, 0:1, :].rearrange("o (p f) -> (o p) f", p=32), in_=cr[:]
-            )
-
-        acc = [
-            psum.tile([P, width], F32, name="acc%d" % u, tag="bk%d" % u)
-            for u, (c0, width) in enumerate(UNITS)
-        ]
-
-        def mx_pass(g, u, rhs):
-            c0, width = UNITS[u]
+        def mx_pass(g, j, rhs):
             nc.tensor.matmul_mx(
-                out=acc[u][:],
+                out=acc[j][:],
                 lhsT=xcodes[:, P * g : P * (g + 1)].bitcast(FP8X4),
                 lhsT_scale=xsc[:, P * g : P * (g + 1)],
                 rhs=rhs.bitcast(FP8X4),
-                rhs_scale=planes[4 * (g % 4) : P, g // 4, c0 : c0 + width],
+                rhs_scale=planes[4 * (g % 4) : P, g // 4, NCH * j : NCH * (j + 1)],
                 start=(g == 0),
                 stop=(g == GROUPS - 1),
             )
 
-        for g in range(FULL):
-            for u, (c0, width) in enumerate(UNITS):
-                mx_pass(g, u, wfull[g][:, 0, c0 : c0 + width])
-        for u, (c0, width) in enumerate(UNITS):
-            if FIRST[u] > FULL:
-                mx_pass(FULL, u, wpart[:, 0, c0 : c0 + width])
+        for g in range(MAIN):
+            for j in range(CHUNKS):
+                mx_pass(g, j, wmain[g][:, NCH * j : NCH * (j + 1)])
+            if g < CHUNKS:
+                cols = slice(NCH * g, NCH * (g + 1))
+                ps = trp.tile([P, NCH], F32, name="ps", tag="tr")
+                nc.tensor.matmul(out=ps[:], lhsT=ones[:], rhs=brow[:, cols], start=True, stop=True)
+                nc.scalar.copy(out=bb[:, cols], in_=ps[:])
 
         out_tok = out[:, 1:65, :].rearrange("b t n -> t b n")
-        for u, (c0, width) in enumerate(UNITS):
-            cols = slice(c0, c0 + width)
-            for g in range(FIRST[u], GROUPS):
-                mx_pass(g, u, wunit[u][:, g - FIRST[u], :])
-            res = rpool.tile([P, width], F32, name="res", tag="res")
-            nc.vector.tensor_tensor(out=res[:], in0=acc[u][:], in1=bb[:, cols], op=ADD)
+        for j in range(CHUNKS):
+            cols = slice(NCH * j, NCH * (j + 1))
+            for g in range(MAIN, GROUPS):
+                mx_pass(g, j, wtail[j][:, g - MAIN, :])
+            res = rpool.tile([P, NCH], F32, name="res")
+            nc.vector.tensor_tensor(out=res[:], in0=acc[j][:], in1=bb[:, cols], op=ADD)
             nc.vector.tensor_tensor(out=res[:], in0=res[:], in1=pos_sb[:, cols], op=MULT)
             nc.sync.dma_start(out=out_tok[:, :, cols], in_=res[:])

@@ -29,8 +29,7 @@ def tile_myvit_w_kernel(tc, X, W_words, W_scales, b, class_token, pos_embed, out
         xpool = ctx.enter_context(tc.tile_pool(name="xpool", bufs=1))
         wpool = ctx.enter_context(tc.tile_pool(name="wpool", bufs=1))
         rpool = ctx.enter_context(tc.tile_pool(name="rpool", bufs=4))
-        accp = ctx.enter_context(tc.psum_pool(name="accp", bufs=1))
-        trp = ctx.enter_context(tc.psum_pool(name="trp", bufs=2))
+        psum = ctx.enter_context(tc.psum_pool(name="psum", bufs=1))
         ctx.enter_context(tc.manual_schedule())
 
         raw0 = xpool.tile([P, 4096], BF16, name="raw0")
@@ -38,6 +37,7 @@ def tile_myvit_w_kernel(tc, X, W_words, W_scales, b, class_token, pos_embed, out
         srt0 = xpool.tile([P, 4096], BF16, name="srt0")
         srt1 = xpool.tile([P, 4096], BF16, name="srt1")
         brow = xpool.tile([P, HID], BF16, name="brow")
+        grouped = xpool.tile([P, GROUPS * P * 4], BF16, name="grouped", align_bytes=64)
         planes = const.tile([P, 3, HID], U8, name="planes", align_bytes=64)
         xcodes = const.tile([P, GROUPS * P], U32, name="xcodes", align_bytes=64)
         xsc = const.tile([P, GROUPS * P], U8, name="xsc", align_bytes=64)
@@ -61,18 +61,12 @@ def tile_myvit_w_kernel(tc, X, W_words, W_scales, b, class_token, pos_embed, out
         nc.sync.dma_start(out=raw0[:], in_=xr[0:128, :])
         nc.sync.dma_start(out=raw1[32:96, :], in_=xr[128:192, :])
 
-        nc.scalar.dma_start(out=ct[:], in_=class_token.rearrange("o (p f) -> (o p) f", p=32))
-        nc.scalar.dma_start(out=p0[:], in_=pos_embed[0:1, :].rearrange("o (p f) -> (o p) f", p=32))
-
         for a in range(3):
             for q in range(4):
-                nc.scalar.dma_start(
+                nc.gpsimd.dma_start(
                     out=planes[32 * q : 32 * q + 16, a, :].bitcast(F32),
                     in_=W_scales[4 * a : 4 * a + 4, 4 * q : 4 * q + 4, :].bitcast(F32),
                 )
-        nc.scalar.dma_start(out=brow[0:1, :], in_=b.rearrange("(o n) -> o n", o=1))
-        nc.sync.dma_start(out=pos_sb[0:128:2, :], in_=pos_embed[1:65, :])
-        nc.sync.dma_start(out=pos_sb[1:128:2, :], in_=pos_embed[1:65, :])
 
         wmain = []
         for g in range(MAIN):
@@ -82,6 +76,16 @@ def tile_myvit_w_kernel(tc, X, W_words, W_scales, b, class_token, pos_embed, out
                 in_=W_words[g].rearrange("p n t -> p (n t)").bitcast(I32),
             )
             wmain.append(w)
+            if g == 1:
+                nc.sync.dma_start(out=brow[0:1, :], in_=b.rearrange("(o n) -> o n", o=1))
+                nc.sync.dma_start(
+                    out=ct[:], in_=class_token.rearrange("o (p f) -> (o p) f", p=32)
+                )
+                nc.sync.dma_start(
+                    out=p0[:], in_=pos_embed[0:1, :].rearrange("o (p f) -> (o p) f", p=32)
+                )
+                nc.sync.dma_start(out=pos_sb[0:128:2, :], in_=pos_embed[1:65, :])
+                nc.sync.dma_start(out=pos_sb[1:128:2, :], in_=pos_embed[1:65, :])
         wtail = []
         for j in range(CHUNKS):
             w = wpool.tile([P, GROUPS - MAIN, NCH], U32, name="wt%d" % j, align_bytes=64)
@@ -104,36 +108,37 @@ def tile_myvit_w_kernel(tc, X, W_words, W_scales, b, class_token, pos_embed, out
         nc.vector.tensor_copy(out=perm1[:, 64:96], in_=ident[:, 0:32])
         nc.vector.tensor_copy(out=perm1[:, 96:128], in_=ident[:, 96:128])
 
-        nc.gpsimd.tensor_tensor(out=cr[:], in0=ct[:], in1=p0[:], op=MULT)
-        for bi in range(2):
-            nc.scalar.dma_start(
-                out=out[bi, 0:1, :].rearrange("o (p f) -> (o p) f", p=32), in_=cr[:]
-            )
-
         for raw, srt in ((raw0, srt0), (raw1, srt1)):
             nc.vector.tensor_copy(
                 out=srt[:].rearrange("q (g y x) -> q g y x", g=8, y=16, x=32),
                 in_=raw[:].rearrange("q (y g x) -> q g y x", y=16, g=8, x=32),
             )
-        grouped = xpool.tile([P, GROUPS * P * 4], BF16, name="grouped", align_bytes=64)
         gw = grouped[:].bitcast(F32).rearrange("p (k x s) -> p k x s", k=96, x=8, s=4)
-        for gx in range(8):
-            ps = trp.tile([P, NCH], F32, name="ps", tag="tr")
+        px = [psum.tile([P, NCH], F32, name="px%d" % gx, tag="bk%d" % gx) for gx in range(8)]
+
+        def transposes(gx, t, srt, perm):
             for u in range(2):
-                for t, (srt, perm) in enumerate(((srt0, perm0), (srt1, perm1))):
-                    slot = 2 * u + t
-                    nc.tensor.transpose(
-                        ps[:, P * slot : P * (slot + 1)],
-                        srt[:].bitcast(F32)[:, 256 * gx + u : 256 * (gx + 1) : 2],
-                        perm[:],
-                    )
+                slot = 2 * u + t
+                nc.tensor.transpose(
+                    px[gx][:, P * slot : P * (slot + 1)],
+                    srt[:].bitcast(F32)[:, 256 * gx + u : 256 * (gx + 1) : 2],
+                    perm[:],
+                )
+
+        for gx in range(8):
+            transposes(gx, 0, srt0, perm0)
+        for gx in range(8):
+            transposes(gx, 1, srt1, perm1)
             src = (
-                ps[:]
+                px[gx][:]
                 .rearrange("p (u r) -> p u r", u=2)[:, :, 0:192]
                 .rearrange("p u (b k) -> p k b u", b=2)
             )
             dst = gw[:, :, gx, :].rearrange("p k (b u) -> p k b u", b=2)
-            nc.vector.tensor_copy(out=dst, in_=src)
+            if (gx // 2) % 2 == 0:
+                nc.vector.tensor_copy(out=dst, in_=src)
+            else:
+                nc.scalar.copy(out=dst, in_=src)
         for i in range(3):
             nc.vector.quantize_mx(
                 out=xcodes[:, 512 * i : 512 * (i + 1)].bitcast(FP8X4),
@@ -141,7 +146,9 @@ def tile_myvit_w_kernel(tc, X, W_words, W_scales, b, class_token, pos_embed, out
                 in_=grouped[:, 2048 * i : 2048 * (i + 1)],
             )
 
-        acc = [accp.tile([P, NCH], F32, name="acc%d" % j) for j in range(CHUNKS)]
+        nc.vector.tensor_tensor(out=cr[:], in0=ct[:], in1=p0[:], op=MULT)
+
+        acc = [psum.tile([P, NCH], F32, name="acc%d" % j, tag="bk%d" % j) for j in range(CHUNKS)]
 
         def mx_pass(g, j, rhs):
             nc.tensor.matmul_mx(
@@ -157,11 +164,15 @@ def tile_myvit_w_kernel(tc, X, W_words, W_scales, b, class_token, pos_embed, out
         for g in range(MAIN):
             for j in range(CHUNKS):
                 mx_pass(g, j, wmain[g][:, NCH * j : NCH * (j + 1)])
-            if g < CHUNKS:
-                cols = slice(NCH * g, NCH * (g + 1))
-                ps = trp.tile([P, NCH], F32, name="ps", tag="tr")
+            if 2 <= g < 2 + CHUNKS:
+                cols = slice(NCH * (g - 2), NCH * (g - 1))
+                ps = psum.tile([P, NCH], F32, name="pb%d" % g, tag="bk%d" % (6 + g % 2))
                 nc.tensor.matmul(out=ps[:], lhsT=ones[:], rhs=brow[:, cols], start=True, stop=True)
                 nc.scalar.copy(out=bb[:, cols], in_=ps[:])
+        for bi in range(2):
+            nc.scalar.dma_start(
+                out=out[bi, 0:1, :].rearrange("o (p f) -> (o p) f", p=32), in_=cr[:]
+            )
 
         out_tok = out[:, 1:65, :].rearrange("b t n -> t b n")
         for j in range(CHUNKS):

@@ -29,15 +29,15 @@ def tile_myvit_w_kernel(tc, X, W_words, W_scales, b, class_token, pos_embed, out
         xpool = ctx.enter_context(tc.tile_pool(name="xpool", bufs=1))
         wpool = ctx.enter_context(tc.tile_pool(name="wpool", bufs=1))
         rpool = ctx.enter_context(tc.tile_pool(name="rpool", bufs=4))
-        psum = ctx.enter_context(tc.psum_pool(name="psum", bufs=1))
+        accp = ctx.enter_context(tc.psum_pool(name="accp", bufs=1))
+        trp = ctx.enter_context(tc.psum_pool(name="trp", bufs=2))
         ctx.enter_context(tc.manual_schedule())
 
         raw0 = xpool.tile([P, 4096], BF16, name="raw0")
         raw1 = xpool.tile([P, 4096], BF16, name="raw1")
         srt0 = xpool.tile([P, 4096], BF16, name="srt0")
         srt1 = xpool.tile([P, 4096], BF16, name="srt1")
-        brow = xpool.tile([P, HID], BF16, name="brow")
-        grouped = xpool.tile([P, GROUPS * P * 4], BF16, name="grouped", align_bytes=64)
+        aux = xpool.tile([P, HID], BF16, name="aux")
         planes = const.tile([P, 3, HID], U8, name="planes", align_bytes=64)
         xcodes = const.tile([P, GROUPS * P], U32, name="xcodes", align_bytes=64)
         xsc = const.tile([P, GROUPS * P], U8, name="xsc", align_bytes=64)
@@ -46,27 +46,33 @@ def tile_myvit_w_kernel(tc, X, W_words, W_scales, b, class_token, pos_embed, out
         ident = const.tile([P, P], F32, name="ident")
         perm0 = const.tile([P, P], F32, name="perm0")
         perm1 = const.tile([P, P], F32, name="perm1")
-        ones = const.tile([P, P], BF16, name="ones")
+        selp = const.tile([P, P], BF16, name="selp")
+        selb = const.tile([P, P], BF16, name="selb")
         ct = const.tile([32, 96], BF16, name="ct")
         p0 = const.tile([32, 96], BF16, name="p0")
         cr = const.tile([32, 96], F32, name="cr")
 
-        nc.vector.memset(planes[:].rearrange("p a n -> p (a n)").bitcast(I32), 0)
         nc.vector.memset(raw1[:].bitcast(I32), 0)
-        nc.vector.memset(brow[:].bitcast(I32), 0)
-        nc.vector.memset(ones[:], 1.0)
+        nc.vector.memset(planes[:].rearrange("p a n -> p (a n)").bitcast(I32), 0)
+        nc.vector.memset(aux[0:32, :].bitcast(I32), 0)
+        nc.vector.memset(aux[96:128, :].bitcast(I32), 0)
         make_identity(nc, ident[:])
 
         xr = X.rearrange("b c (r y) x -> (b c r) (y x)", y=16)
         nc.sync.dma_start(out=raw0[:], in_=xr[0:128, :])
         nc.sync.dma_start(out=raw1[32:96, :], in_=xr[128:192, :])
 
+        nc.scalar.dma_start(out=ct[:], in_=class_token.rearrange("o (p f) -> (o p) f", p=32))
+        nc.scalar.dma_start(out=p0[:], in_=pos_embed[0:1, :].rearrange("o (p f) -> (o p) f", p=32))
+        nc.scalar.dma_start(out=aux[0:1, :], in_=b.rearrange("(o n) -> o n", o=1))
+
         for a in range(3):
             for q in range(4):
-                nc.gpsimd.dma_start(
-                    out=planes[32 * q : 32 * q + 16, a, :].bitcast(F32),
-                    in_=W_scales[4 * a : 4 * a + 4, 4 * q : 4 * q + 4, :].bitcast(F32),
+                nc.sync.dma_start(
+                    out=planes[32 * q : 32 * q + 16, a, :].bitcast(I32),
+                    in_=W_scales[4 * a : 4 * a + 4, 4 * q : 4 * q + 4, :].bitcast(I32),
                 )
+        nc.sync.dma_start(out=aux[32:96, :], in_=pos_embed[1:65, :])
 
         wmain = []
         for g in range(MAIN):
@@ -76,16 +82,6 @@ def tile_myvit_w_kernel(tc, X, W_words, W_scales, b, class_token, pos_embed, out
                 in_=W_words[g].rearrange("p n t -> p (n t)").bitcast(I32),
             )
             wmain.append(w)
-            if g == 1:
-                nc.sync.dma_start(out=brow[0:1, :], in_=b.rearrange("(o n) -> o n", o=1))
-                nc.sync.dma_start(
-                    out=ct[:], in_=class_token.rearrange("o (p f) -> (o p) f", p=32)
-                )
-                nc.sync.dma_start(
-                    out=p0[:], in_=pos_embed[0:1, :].rearrange("o (p f) -> (o p) f", p=32)
-                )
-                nc.sync.dma_start(out=pos_sb[0:128:2, :], in_=pos_embed[1:65, :])
-                nc.sync.dma_start(out=pos_sb[1:128:2, :], in_=pos_embed[1:65, :])
         wtail = []
         for j in range(CHUNKS):
             w = wpool.tile([P, GROUPS - MAIN, NCH], U32, name="wt%d" % j, align_bytes=64)
@@ -107,30 +103,37 @@ def tile_myvit_w_kernel(tc, X, W_words, W_scales, b, class_token, pos_embed, out
         )
         nc.vector.tensor_copy(out=perm1[:, 64:96], in_=ident[:, 0:32])
         nc.vector.tensor_copy(out=perm1[:, 96:128], in_=ident[:, 96:128])
+        nc.vector.tensor_copy(
+            out=selp[:].rearrange("p (t b) -> p t b", b=2),
+            in_=ident[:, 32:96].unsqueeze(2).to_broadcast([P, 64, 2]),
+        )
+        nc.vector.tensor_copy(out=selb[:], in_=ident[:, 0:1].to_broadcast([P, P]))
+
+        nc.gpsimd.tensor_tensor(out=cr[:], in0=ct[:], in1=p0[:], op=MULT)
+        for bi in range(2):
+            nc.scalar.dma_start(
+                out=out[bi, 0:1, :].rearrange("o (p f) -> (o p) f", p=32), in_=cr[:]
+            )
 
         for raw, srt in ((raw0, srt0), (raw1, srt1)):
             nc.vector.tensor_copy(
                 out=srt[:].rearrange("q (g y x) -> q g y x", g=8, y=16, x=32),
                 in_=raw[:].rearrange("q (y g x) -> q g y x", y=16, g=8, x=32),
             )
+        grouped = xpool.tile([P, GROUPS * P * 4], BF16, name="grouped", align_bytes=64)
         gw = grouped[:].bitcast(F32).rearrange("p (k x s) -> p k x s", k=96, x=8, s=4)
-        px = [psum.tile([P, NCH], F32, name="px%d" % gx, tag="bk%d" % gx) for gx in range(8)]
-
-        def transposes(gx, t, srt, perm):
+        for gx in range(8):
+            ps = trp.tile([P, NCH], F32, name="ps", tag="tr")
             for u in range(2):
-                slot = 2 * u + t
-                nc.tensor.transpose(
-                    px[gx][:, P * slot : P * (slot + 1)],
-                    srt[:].bitcast(F32)[:, 256 * gx + u : 256 * (gx + 1) : 2],
-                    perm[:],
-                )
-
-        for gx in range(8):
-            transposes(gx, 0, srt0, perm0)
-        for gx in range(8):
-            transposes(gx, 1, srt1, perm1)
+                for t, (srt, perm) in enumerate(((srt0, perm0), (srt1, perm1))):
+                    slot = 2 * u + t
+                    nc.tensor.transpose(
+                        ps[:, P * slot : P * (slot + 1)],
+                        srt[:].bitcast(F32)[:, 256 * gx + u : 256 * (gx + 1) : 2],
+                        perm[:],
+                    )
             src = (
-                px[gx][:]
+                ps[:]
                 .rearrange("p (u r) -> p u r", u=2)[:, :, 0:192]
                 .rearrange("p u (b k) -> p k b u", b=2)
             )
@@ -146,9 +149,7 @@ def tile_myvit_w_kernel(tc, X, W_words, W_scales, b, class_token, pos_embed, out
                 in_=grouped[:, 2048 * i : 2048 * (i + 1)],
             )
 
-        nc.vector.tensor_tensor(out=cr[:], in0=ct[:], in1=p0[:], op=MULT)
-
-        acc = [psum.tile([P, NCH], F32, name="acc%d" % j, tag="bk%d" % j) for j in range(CHUNKS)]
+        acc = [accp.tile([P, NCH], F32, name="acc%d" % j) for j in range(CHUNKS)]
 
         def mx_pass(g, j, rhs):
             nc.tensor.matmul_mx(
@@ -164,15 +165,12 @@ def tile_myvit_w_kernel(tc, X, W_words, W_scales, b, class_token, pos_embed, out
         for g in range(MAIN):
             for j in range(CHUNKS):
                 mx_pass(g, j, wmain[g][:, NCH * j : NCH * (j + 1)])
-            if 2 <= g < 2 + CHUNKS:
-                cols = slice(NCH * (g - 2), NCH * (g - 1))
-                ps = psum.tile([P, NCH], F32, name="pb%d" % g, tag="bk%d" % (6 + g % 2))
-                nc.tensor.matmul(out=ps[:], lhsT=ones[:], rhs=brow[:, cols], start=True, stop=True)
-                nc.scalar.copy(out=bb[:, cols], in_=ps[:])
-        for bi in range(2):
-            nc.scalar.dma_start(
-                out=out[bi, 0:1, :].rearrange("o (p f) -> (o p) f", p=32), in_=cr[:]
-            )
+            if g < CHUNKS:
+                cols = slice(NCH * g, NCH * (g + 1))
+                for sel, wide in ((selb, bb), (selp, pos_sb)):
+                    ps = trp.tile([P, NCH], F32, name="ps", tag="tr")
+                    nc.tensor.matmul(out=ps[:], lhsT=sel[:], rhs=aux[:, cols], start=True, stop=True)
+                    nc.scalar.copy(out=wide[:, cols], in_=ps[:])
 
         out_tok = out[:, 1:65, :].rearrange("b t n -> t b n")
         for j in range(CHUNKS):

from contextlib import ExitStack

import concourse.mybir as mybir
from concourse.masks import make_identity

F32 = mybir.dt.float32
BF16 = mybir.dt.bfloat16
I32 = mybir.dt.int32
U32 = mybir.dt.uint32
U8 = mybir.dt.uint8
FP8X4 = mybir.dt.float8_e4m3fn_x4
ADD = mybir.AluOpType.add
MULT = mybir.AluOpType.mult

P = 128
HID = 3072
GROUPS = 12
NCH = 512
CHUNKS = HID // NCH
MAIN = 10

FLOPS = 2 * 128 * 6144 * 3072


def tile_myvit_w_kernel(tc, X, W_words, W_scales, b, class_token, pos_embed, out):
    nc = tc.nc
    with ExitStack() as ctx:
        const = ctx.enter_context(tc.tile_pool(name="const", bufs=1))
        xpool = ctx.enter_context(tc.tile_pool(name="xpool", bufs=1))
        wpool = ctx.enter_context(tc.tile_pool(name="wpool", bufs=1))
        rpool = ctx.enter_context(tc.tile_pool(name="rpool", bufs=4))
        accp = ctx.enter_context(tc.psum_pool(name="accp", bufs=1))
        trp = ctx.enter_context(tc.psum_pool(name="trp", bufs=2))
        ctx.enter_context(tc.manual_schedule())

        raw0 = xpool.tile([P, 4096], BF16, name="raw0")
        raw1 = xpool.tile([P, 4096], BF16, name="raw1")
        srt0 = xpool.tile([P, 4096], BF16, name="srt0")
        srt1 = xpool.tile([P, 4096], BF16, name="srt1")
        aux = xpool.tile([P, HID], BF16, name="aux")
        planes = const.tile([P, 3, HID], U8, name="planes", align_bytes=64)
        xcodes = const.tile([P, GROUPS * P], U32, name="xcodes", align_bytes=64)
        xsc = const.tile([P, GROUPS * P], U8, name="xsc", align_bytes=64)
        pos_sb = const.tile([P, HID], BF16, name="pos_sb")
        bb = const.tile([P, HID], BF16, name="bb")
        ident = const.tile([P, P], F32, name="ident")
        perm0 = const.tile([P, P], F32, name="perm0")
        perm1 = const.tile([P, P], F32, name="perm1")
        selp = const.tile([P, P], BF16, name="selp")
        selb = const.tile([P, P], BF16, name="selb")
        ct = const.tile([32, 96], BF16, name="ct")
        p0 = const.tile([32, 96], BF16, name="p0")
        cr = const.tile([32, 96], F32, name="cr")

        nc.vector.memset(raw1[:].bitcast(I32), 0)
        nc.vector.memset(planes[:].rearrange("p a n -> p (a n)").bitcast(I32), 0)
        nc.vector.memset(aux[0:32, :].bitcast(I32), 0)
        nc.vector.memset(aux[96:128, :].bitcast(I32), 0)
        make_identity(nc, ident[:])

        xr = X.rearrange("b c (r y) x -> (b c r) (y x)", y=16)
        nc.sync.dma_start(out=raw0[:], in_=xr[0:128, :])
        nc.sync.dma_start(out=raw1[32:96, :], in_=xr[128:192, :])

        nc.scalar.dma_start(out=ct[:], in_=class_token.rearrange("o (p f) -> (o p) f", p=32))
        nc.scalar.dma_start(out=p0[:], in_=pos_embed[0:1, :].rearrange("o (p f) -> (o p) f", p=32))
        nc.scalar.dma_start(out=aux[0:1, :], in_=b.rearrange("(o n) -> o n", o=1))

        for a in range(3):
            for q in range(4):
                nc.sync.dma_start(
                    out=planes[32 * q : 32 * q + 16, a, :].bitcast(I32),
                    in_=W_scales[4 * a : 4 * a + 4, 4 * q : 4 * q + 4, :].bitcast(I32),
                )
        nc.sync.dma_start(out=aux[32:96, :], in_=pos_embed[1:65, :])

        wmain = []
        for g in range(MAIN):
            w = wpool.tile([P, HID], U32, name="w%d" % g, align_bytes=64)
            nc.sync.dma_start(
                out=w[:].bitcast(I32),
                in_=W_words[g].rearrange("p n t -> p (n t)").bitcast(I32),
            )
            wmain.append(w)
        wtail = []
        for j in range(CHUNKS):
            w = wpool.tile([P, GROUPS - MAIN, NCH], U32, name="wt%d" % j, align_bytes=64)
            nc.sync.dma_start(
                out=w[:].bitcast(I32),
                in_=W_words[MAIN:GROUPS, :, NCH * j : NCH * (j + 1), :]
                .rearrange("g p n t -> p g (n t)")
                .bitcast(I32),
            )
            wtail.append(w)

        nc.vector.tensor_copy(
            out=perm0[:].rearrange("p (c h y) -> p c h y", c=8, h=2, y=8),
            in_=ident[:].rearrange("p (c y h) -> p c h y", c=8, y=8, h=2),
        )
        nc.vector.tensor_copy(
            out=perm1[:, 0:64].rearrange("p (c h y) -> p c h y", c=4, h=2, y=8),
            in_=ident[:, 32:96].rearrange("p (c y h) -> p c h y", c=4, y=8, h=2),
        )
        nc.vector.tensor_copy(out=perm1[:, 64:96], in_=ident[:, 0:32])
        nc.vector.tensor_copy(out=perm1[:, 96:128], in_=ident[:, 96:128])
        nc.vector.tensor_copy(
            out=selp[:].rearrange("p (t b) -> p t b", b=2),
            in_=ident[:, 32:96].unsqueeze(2).to_broadcast([P, 64, 2]),
        )
        nc.vector.tensor_copy(out=selb[:], in_=ident[:, 0:1].to_broadcast([P, P]))

        nc.gpsimd.tensor_tensor(out=cr[:], in0=ct[:], in1=p0[:], op=MULT)
        for bi in range(2):
            nc.scalar.dma_start(
                out=out[bi, 0:1, :].rearrange("o (p f) -> (o p) f", p=32), in_=cr[:]
            )

        for raw, srt in ((raw0, srt0), (raw1, srt1)):
            nc.vector.tensor_copy(
                out=srt[:].rearrange("q (g y x) -> q g y x", g=8, y=16, x=32),
                in_=raw[:].rearrange("q (y g x) -> q g y x", y=16, g=8, x=32),
            )
        grouped = xpool.tile([P, GROUPS * P * 4], BF16, name="grouped", align_bytes=64)
        gw = grouped[:].bitcast(F32).rearrange("p (k x s) -> p k x s", k=96, x=8, s=4)
        for gx in range(8):
            ps = trp.tile([P, NCH], F32, name="ps", tag="tr")
            for u in range(2):
                for t, (srt, perm) in enumerate(((srt0, perm0), (srt1, perm1))):
                    slot = 2 * u + t
                    nc.tensor.transpose(
                        ps[:, P * slot : P * (slot + 1)],
                        srt[:].bitcast(F32)[:, 256 * gx + u : 256 * (gx + 1) : 2],
                        perm[:],
                    )
            src = (
                ps[:]
                .rearrange("p (u r) -> p u r", u=2)[:, :, 0:192]
                .rearrange("p u (b k) -> p k b u", b=2)
            )
            dst = gw[:, :, gx, :].rearrange("p k (b u) -> p k b u", b=2)
            if (gx // 2) % 2 == 0:
                nc.vector.tensor_copy(out=dst, in_=src)
            else:
                nc.scalar.copy(out=dst, in_=src)
        for i in range(3):
            nc.vector.quantize_mx(
                out=xcodes[:, 512 * i : 512 * (i + 1)].bitcast(FP8X4),
                scales=xsc[:, 512 * i : 512 * (i + 1)],
                in_=grouped[:, 2048 * i : 2048 * (i + 1)],
            )

        acc = [accp.tile([P, NCH], F32, name="acc%d" % j) for j in range(CHUNKS)]

        def mx_pass(g, j, rhs):
            nc.tensor.matmul_mx(
                out=acc[j][:],
                lhsT=xcodes[:, P * g : P * (g + 1)].bitcast(FP8X4),
                lhsT_scale=xsc[:, P * g : P * (g + 1)],
                rhs=rhs.bitcast(FP8X4),
                rhs_scale=planes[4 * (g % 4) : P, g // 4, NCH * j : NCH * (j + 1)],
                start=(g == 0),
                stop=(g == GROUPS - 1),
            )

        for g in range(MAIN):
            for j in range(CHUNKS):
                mx_pass(g, j, wmain[g][:, NCH * j : NCH * (j + 1)])
            if g < CHUNKS:
                cols = slice(NCH * g, NCH * (g + 1))
                for sel, wide in ((selb, bb), (selp, pos_sb)):
                    ps = trp.tile([P, NCH], F32, name="ps", tag="tr")
                    nc.tensor.matmul(out=ps[:], lhsT=sel[:], rhs=aux[:, cols], start=True, stop=True)
                    nc.scalar.copy(out=wide[:, cols], in_=ps[:])

        out_tok = out[:, 1:65, :].rearrange("b t n -> t b n")
        for j in range(CHUNKS):
            cols = slice(NCH * j, NCH * (j + 1))
            for g in range(MAIN, GROUPS):
                mx_pass(g, j, wtail[j][:, g - MAIN, :])
            res = rpool.tile([P, NCH], F32, name="res")
            nc.vector.tensor_tensor(out=res[:], in0=acc[j][:], in1=bb[:, cols], op=ADD)
            nc.vector.tensor_tensor(out=res[:], in0=res[:], in1=pos_sb[:, cols], op=MULT)
            nc.sync.dma_start(out=out_tok[:, :, cols], in_=res[:])
